import numpy as np
import ml_dtypes


def mxq(x, axis, fmt="e4m3"):
    dtype, down = {"e4m3": (ml_dtypes.float8_e4m3fn, 7), "e5m2": (ml_dtypes.float8_e5m2, 14)}[fmt]
    v = np.moveaxis(np.asarray(x, np.float32).astype(ml_dtypes.bfloat16).astype(np.float64), axis, -1)
    blocks = v.reshape(v.shape[:-1] + (-1, 32))
    amax = np.abs(blocks).max(-1, keepdims=True)
    byte = np.maximum(np.where(amax > 0, np.frexp(amax)[1] - 1 + 127, 0) - down, 1)
    scale = np.exp2(byte - 127.0)
    codes = (blocks / scale).astype(np.float32).astype(dtype).astype(np.float64)
    return np.moveaxis((codes * scale).reshape(v.shape), -1, axis)


WIDE = False


def mx_kscale(k):
    if not WIDE:
        return np.ones(k)
    levels = np.array([10, -10, 5, -5, 0])
    a = np.random.permutation(np.resize(levels, k // 512 * 4)).reshape(k // 512, 4)
    idx = np.arange(k)
    return np.exp2(a[idx // 512, idx % 128 // 32])


BF16 = ml_dtypes.bfloat16


def bf(x):
    return np.asarray(x, np.float32).astype(BF16)


def f64(x):
    return np.asarray(x).astype(np.float64)


B, C, HH, WW = 8, 512, 28, 28
BN_EPS = 1e-5


def ch(v):
    return v[None, :, None, None]


def setup_inputs():
    u = mx_kscale(C)
    return {"x": bf(np.random.standard_normal((B, C, HH, WW))),
            "rsign_bias": bf(0.1 * np.random.standard_normal(C)),
            "W": bf(np.random.standard_normal((C, C)) * 1.1 / np.sqrt(C) * u[:, None]),
            "bn_gamma": bf((1.0 + 0.1 * np.random.standard_normal(C)) / u),
            "bn_beta": bf(0.1 * np.random.standard_normal(C)),
            "bn_mean": bf(0.1 * np.random.standard_normal(C) * u),
            "bn_var": bf(np.random.uniform(0.5, 1.5, C)),
            "pr_slope": bf(np.random.uniform(0.1, 0.35, C)),
            "pr_shift": bf(0.1 * np.random.standard_normal(C)),
            "pr_bias": bf(0.1 * np.random.standard_normal(C))}


def reference(x, rsign_bias, W, bn_gamma, bn_beta, bn_mean, bn_var, pr_slope, pr_shift, pr_bias):
    x = f64(x)
    W = f64(W)
    a = np.sign(x + ch(f64(rsign_bias)))
    scale = np.mean(np.abs(W), axis=1)
    Wb = np.sign(W) * scale[:, None]
    y = (mxq(Wb, 1, "e4m3") @ mxq(a, 1, "e4m3").reshape(B, C, HH * WW)).reshape(B, C, HH, WW)
    bn = ch(f64(bn_gamma)) * (y - ch(f64(bn_mean))) * (1.0 / np.sqrt(ch(f64(bn_var)) + BN_EPS)) + ch(f64(bn_beta))
    s = bn + x
    t = s - ch(f64(pr_shift))
    return np.where(t > 0, t, ch(f64(pr_slope)) * t) + ch(f64(pr_bias))

@@ -1,0 +1,222 @@
+from contextlib import ExitStack
+
+import concourse.mybir as mybir
+from concourse.masks import make_identity
+
+F32 = mybir.dt.float32
+BF16 = mybir.dt.bfloat16
+U32 = mybir.dt.uint32
+U8 = mybir.dt.uint8
+FP8X4 = mybir.dt.float8_e4m3fn_x4
+ACT = mybir.ActivationFunctionType
+ALU = mybir.AluOpType
+
+P = 128
+J = 4
+B = 8
+C = 512
+HW = 784
+PADW = 896
+BN_EPS = 1e-5
+FLOPS = 2 * C * C * B * HW
+
+
+def tile_lowerblock_kernel(
+    tc, x, rsign_bias, W, bn_gamma, bn_beta, bn_mean, bn_var, pr_slope, pr_shift, pr_bias, out
+):
+    nc = tc.nc
+    x_v = x.rearrange("b (p j) h w -> b p j (h w)", j=J)
+    out_v = out.rearrange("b (p j) h w -> b p j (h w)", j=J)
+
+    with ExitStack() as ctx:
+        consts = ctx.enter_context(tc.tile_pool(name="consts", bufs=1))
+        xpool = ctx.enter_context(tc.tile_pool(name="xpool", bufs=B))
+        dpool = ctx.enter_context(tc.tile_pool(name="dpool", bufs=2))
+        zpool = ctx.enter_context(tc.tile_pool(name="zpool", bufs=4))
+        qpool = ctx.enter_context(tc.tile_pool(name="qpool", bufs=2))
+        psum = ctx.enter_context(tc.psum_pool(name="psum", bufs=8))
+
+        def vec_tile(name):
+            return consts.tile([P, J], BF16, name=name)
+
+        def vec_view(v):
+            return v.rearrange("(p j) -> p j", j=J)
+
+        var_b = vec_tile("var_b")
+        rb_b = vec_tile("rb_b")
+        gam_b = vec_tile("gam_b")
+        mean_b = vec_tile("mean_b")
+        beta_b = vec_tile("beta_b")
+        shift_b = vec_tile("shift_b")
+        pb_b = vec_tile("pb_b")
+        slope_b = vec_tile("slope_b")
+        ident = consts.tile([P, P], BF16, name="ident")
+        make_identity(nc, ident[:])
+
+        w_sb = consts.tile([P, J, C], BF16, name="w_sb")
+        x_t = []
+        for b in range(B):
+            xt = xpool.tile([P, J, HW], BF16, name="xt")
+            x_t.append(xt)
+        nc.scalar.dma_start(out=var_b[:], in_=vec_view(bn_var))
+        nc.sync.dma_start(out=w_sb[:], in_=W.rearrange("(p j) i -> p j i", j=J))
+        nc.sync.dma_start(out=x_t[0][:], in_=x_v[0])
+        nc.scalar.dma_start(out=rb_b[:], in_=vec_view(rsign_bias))
+        nc.scalar.dma_start(out=gam_b[:], in_=vec_view(bn_gamma))
+        nc.scalar.dma_start(out=mean_b[:], in_=vec_view(bn_mean))
+        nc.scalar.dma_start(out=beta_b[:], in_=vec_view(bn_beta))
+        nc.scalar.dma_start(out=shift_b[:], in_=vec_view(pr_shift))
+        nc.scalar.dma_start(out=pb_b[:], in_=vec_view(pr_bias))
+        nc.scalar.dma_start(out=slope_b[:], in_=vec_view(pr_slope))
+        for b in range(1, B):
+            nc.sync.dma_start(out=x_t[b][:], in_=x_v[b])
+
+        grp = []
+        for g in range(2):
+            gt = consts.tile([P, PADW, J], BF16, name="grp%d" % g, align_bytes=64)
+            nc.vector.memset(gt[:, HW:PADW, :], 0.0)
+            grp.append(gt)
+
+        ve = consts.tile([P, J], F32, name="ve")
+        nc.vector.tensor_scalar(out=ve[:], in0=var_b[:], scalar1=BN_EPS, scalar2=None, op0=ALU.add)
+        sq = consts.tile([P, J], F32, name="sq")
+        nc.scalar.activation(out=sq[:], in_=ve[:], func=ACT.Sqrt)
+        rstd = consts.tile([P, J], F32, name="rstd")
+        nc.vector.reciprocal(out=rstd[:], in_=sq[:])
+        a_c = consts.tile([P, J], F32, name="a_c")
+        nc.vector.tensor_tensor(out=a_c[:], in0=gam_b[:], in1=rstd[:], op=ALU.mult)
+        am = consts.tile([P, J], F32, name="am")
+        nc.vector.tensor_tensor(out=am[:], in0=a_c[:], in1=mean_b[:], op=ALU.mult)
+        k1 = consts.tile([P, J], F32, name="k1")
+        nc.vector.tensor_tensor(out=k1[:], in0=beta_b[:], in1=am[:], op=ALU.subtract)
+        k2 = consts.tile([P, J], F32, name="k2")
+        nc.vector.tensor_tensor(out=k2[:], in0=k1[:], in1=shift_b[:], op=ALU.subtract)
+        k_c = consts.tile([P, J], F32, name="k_c")
+        nc.vector.tensor_tensor(out=k_c[:], in0=k2[:], in1=pb_b[:], op=ALU.add)
+        pb_c = consts.tile([P, J], F32, name="pb_c")
+        nc.vector.tensor_copy(out=pb_c[:], in_=pb_b[:])
+        c_c = consts.tile([P, J], F32, name="c_c")
+        nc.vector.tensor_scalar(
+            out=c_c[:], in0=slope_b[:], scalar1=-1.0, scalar2=1.0, op0=ALU.mult, op1=ALU.add
+        )
+
+        wmean = consts.tile([P, J], F32, name="wmean")
+        wabs = consts.tile([P, C], BF16, name="wabs")
+        sgn = consts.tile([P, J, C], BF16, name="sgn")
+        wb = consts.tile([P, J, J, P], BF16, name="wb")
+        g_w = consts.tile([P, J, P, J], BF16, name="g_w", align_bytes=64)
+        w_codes = consts.tile([P, C], U32, name="w_codes", align_bytes=64)
+        w_scl = consts.tile([P, C], U8, name="w_scl", align_bytes=64)
+        w_flat = w_sb[:].rearrange("p j i -> p (j i)")
+        w_gt = consts.tile([P, J * C], BF16, name="w_gt")
+        w_lt = consts.tile([P, J * C], BF16, name="w_lt")
+        nc.vector.tensor_scalar(out=w_gt[:], in0=w_flat, scalar1=0.0, scalar2=None, op0=ALU.is_gt)
+        nc.vector.tensor_scalar(out=w_lt[:], in0=w_flat, scalar1=0.0, scalar2=None, op0=ALU.is_lt)
+        nc.vector.tensor_tensor(
+            out=sgn[:].rearrange("p j i -> p (j i)"), in0=w_gt[:], in1=w_lt[:], op=ALU.subtract
+        )
+        for j in range(J):
+            nc.scalar.activation(
+                out=wabs[:], in_=w_sb[:, j, :], func=ACT.Abs, scale=1.0 / C,
+                accum_out=wmean[:, j : j + 1],
+            )
+        for j in range(J):
+            nc.vector.tensor_scalar(
+                out=wb[:, j], in0=sgn[:, j, :].rearrange("p (q t) -> p t q", t=J),
+                scalar1=wmean[:, j : j + 1], scalar2=None, op0=ALU.mult,
+            )
+            wT = psum.tile([P, J, P], BF16, name="wT", tag="acc")
+            for t in range(J):
+                nc.tensor.transpose(wT[:, t, :], wb[:, j, t, :], ident[:])
+            nc.vector.tensor_copy(out=g_w[:, j], in_=wT[:].rearrange("p t r -> p r t"))
+        for j in range(J):
+            cols = slice(j * P, (j + 1) * P)
+            nc.vector.quantize_mx(
+                out=w_codes[:, cols].bitcast(FP8X4),
+                scales=w_scl[:, cols],
+                in_=g_w[:, j].rearrange("p r t -> p (r t)"),
+            )
+
+        codes = consts.tile([P, B, PADW], U32, name="codes", align_bytes=64)
+        scl = consts.tile([P, B, PADW], U8, name="scl", align_bytes=64)
+        z_t = {}
+
+        def front(b):
+            xt = x_t[b]
+            dt_ = dpool.tile([P, J, HW], BF16, name="dt_")
+            for j in range(J):
+                nc.vector.tensor_scalar(
+                    out=dt_[:, j, :], in0=xt[:, j, :], scalar1=rb_b[:, j : j + 1], scalar2=None,
+                    op0=ALU.add,
+                )
+            gt = grp[b % 2]
+            for c0, c1 in ((0, 512), (512, HW)):
+                nc.scalar.activation(
+                    out=gt[:, c0:c1, :].rearrange("p (c i) t -> p c t i", i=4),
+                    in_=dt_[:, :, c0:c1].rearrange("p t (c i) -> p c t i", i=4),
+                    func=ACT.Sign,
+                )
+            flat = gt[:].rearrange("p w t -> p (w t)")
+            for c0, c1 in ((0, 512), (512, 768), (768, 896)):
+                nc.vector.quantize_mx(
+                    out=codes[:, b, c0:c1].bitcast(FP8X4),
+                    scales=scl[:, b, c0:c1],
+                    in_=flat[:, 4 * c0 : 4 * c1],
+                )
+            zt = zpool.tile([P, J, HW], F32, name="zt")
+            for j in range(J):
+                nc.gpsimd.tensor_scalar(
+                    out=zt[:, j, :], in0=xt[:, j, :], scalar1=1.0, scalar2=k_c[:, j : j + 1],
+                    op0=ALU.mult, op1=ALU.add,
+                )
+            z_t[b] = zt
+
+        def mx(acc, j, b, c0, c1):
+            wcols = slice(j * P, (j + 1) * P)
+            nc.tensor.matmul_mx(
+                out=acc,
+                lhsT=w_codes[:, wcols].bitcast(FP8X4),
+                lhsT_scale=w_scl[:, wcols],
+                rhs=codes[:, b, c0:c1].bitcast(FP8X4),
+                rhs_scale=scl[:, b, c0:c1],
+                start=True,
+                stop=True,
+            )
+
+        def back(b):
+            zt = z_t[b]
+            qt = qpool.tile([P, J, HW], F32, name="qt")
+            for j in range(J):
+                acc_a = psum.tile([P, 512], F32, name="acc_a", tag="acc")
+                acc_b = psum.tile([P, 512], F32, name="acc_b", tag="acc")
+                mx(acc_a[:], j, b, 0, 512)
+                mx(acc_b[:, 0:256], j, b, 512, 768)
+                mx(acc_b[:, 256:384], j, b, 768, 896)
+                nc.vector.scalar_tensor_tensor(
+                    out=zt[:, j, 0:512], in0=acc_a[:], scalar=a_c[:, j : j + 1],
+                    in1=zt[:, j, 0:512], op0=ALU.mult, op1=ALU.add,
+                )
+                nc.vector.scalar_tensor_tensor(
+                    out=zt[:, j, 512:HW], in0=acc_b[:, 0 : HW - 512], scalar=a_c[:, j : j + 1],
+                    in1=zt[:, j, 512:HW], op0=ALU.mult, op1=ALU.add,
+                )
+                nc.scalar.activation(
+                    out=qt[:, j, :], in_=zt[:, j, :], func=ACT.Relu, bias=pb_c[:, j : j + 1],
+                    scale=-1.0,
+                )
+            for j in range(J):
+                nc.vector.scalar_tensor_tensor(
+                    out=zt[:, j, :], in0=qt[:, j, :], scalar=c_c[:, j : j + 1],
+                    in1=zt[:, j, :], op0=ALU.mult, op1=ALU.add,
+                )
+                if b == B - 1:
+                    nc.sync.dma_start(out=out_v[b][:, j, :], in_=zt[:, j, :])
+            if b < B - 1:
+                nc.sync.dma_start(out=out_v[b], in_=zt[:])
+
+        front(0)
+        front(1)
+        for b in range(B):
+            if b + 2 < B:
+                front(b + 2)
+            back(b)

@@ -165,10 +165,16 @@ def tile_lowerblock_kernel(
                 )
             zt = zpool.tile([P, J, HW], F32, name="zt")
             for j in range(J):
-                nc.gpsimd.tensor_scalar(
-                    out=zt[:, j, :], in0=xt[:, j, :], scalar1=1.0, scalar2=k_c[:, j : j + 1],
-                    op0=ALU.mult, op1=ALU.add,
-                )
+                if b < 4:
+                    nc.vector.tensor_scalar(
+                        out=zt[:, j, :], in0=xt[:, j, :], scalar1=k_c[:, j : j + 1], scalar2=None,
+                        op0=ALU.add,
+                    )
+                else:
+                    nc.scalar.activation(
+                        out=zt[:, j, :], in_=xt[:, j, :], func=ACT.Identity,
+                        bias=k_c[:, j : j + 1], scale=1.0,
+                    )
             z_t[b] = zt
 
         def mx(acc, j, b, c0, c1):

@@ -16,7 +16,9 @@ J = 4
 B = 8
 C = 512
 HW = 784
-PADW = 896
+N = B * HW
+CHUNKS = (512, 1024, 1024, 1024, 1024, 1024, 640)
+G_UNITS = 3
 BN_EPS = 1e-5
 FLOPS = 2 * C * C * B * HW
 
@@ -27,99 +29,187 @@ def tile_lowerblock_kernel(
     nc = tc.nc
     x_v = x.rearrange("b (p j) h w -> b p j (h w)", j=J)
     out_v = out.rearrange("b (p j) h w -> b p j (h w)", j=J)
+    n_chunks = len(CHUNKS)
+    starts = [sum(CHUNKS[:k]) for k in range(n_chunks)]
+
+    def pieces(width):
+        cuts = list(range(0, width, 512)) + [width]
+        return list(zip(cuts[:-1], cuts[1:]))
 
     with ExitStack() as ctx:
         consts = ctx.enter_context(tc.tile_pool(name="consts", bufs=1))
-        xpool = ctx.enter_context(tc.tile_pool(name="xpool", bufs=B))
         dpool = ctx.enter_context(tc.tile_pool(name="dpool", bufs=2))
+        gpool = ctx.enter_context(tc.tile_pool(name="gpool", bufs=2))
         zpool = ctx.enter_context(tc.tile_pool(name="zpool", bufs=4))
-        qpool = ctx.enter_context(tc.tile_pool(name="qpool", bufs=2))
+        qpool = ctx.enter_context(tc.tile_pool(name="qpool", bufs=6))
         psum = ctx.enter_context(tc.psum_pool(name="psum", bufs=8))
+        ctx.enter_context(tc.manual_schedule())
 
-        def vec_tile(name):
-            return consts.tile([P, J], BF16, name=name)
+        def vec_load(queue, v, name):
+            t = consts.tile([P, J], BF16, name=name)
+            queue.dma_start(out=t[:], in_=v.rearrange("(p j) -> p j", j=J))
+            return t
 
-        def vec_view(v):
-            return v.rearrange("(p j) -> p j", j=J)
-
-        var_b = vec_tile("var_b")
-        rb_b = vec_tile("rb_b")
-        gam_b = vec_tile("gam_b")
-        mean_b = vec_tile("mean_b")
-        beta_b = vec_tile("beta_b")
-        shift_b = vec_tile("shift_b")
-        pb_b = vec_tile("pb_b")
-        slope_b = vec_tile("slope_b")
+        shift_b = vec_load(nc.gpsimd, pr_shift, "shift_b")
+        pb_b = vec_load(nc.gpsimd, pr_bias, "pb_b")
+        slope_b = vec_load(nc.gpsimd, pr_slope, "slope_b")
         ident = consts.tile([P, P], BF16, name="ident")
         make_identity(nc, ident[:])
 
+        var_b = vec_load(nc.scalar, bn_var, "var_b")
         w_sb = consts.tile([P, J, C], BF16, name="w_sb")
-        x_t = []
-        for b in range(B):
-            xt = xpool.tile([P, J, HW], BF16, name="xt")
-            x_t.append(xt)
-        nc.scalar.dma_start(out=var_b[:], in_=vec_view(bn_var))
+        x_sb = consts.tile([P, J, N], BF16, name="x_sb")
         nc.sync.dma_start(out=w_sb[:], in_=W.rearrange("(p j) i -> p j i", j=J))
-        nc.sync.dma_start(out=x_t[0][:], in_=x_v[0])
-        nc.scalar.dma_start(out=rb_b[:], in_=vec_view(rsign_bias))
-        nc.scalar.dma_start(out=gam_b[:], in_=vec_view(bn_gamma))
-        nc.scalar.dma_start(out=mean_b[:], in_=vec_view(bn_mean))
-        nc.scalar.dma_start(out=beta_b[:], in_=vec_view(bn_beta))
-        nc.scalar.dma_start(out=shift_b[:], in_=vec_view(pr_shift))
-        nc.scalar.dma_start(out=pb_b[:], in_=vec_view(pr_bias))
-        nc.scalar.dma_start(out=slope_b[:], in_=vec_view(pr_slope))
+        nc.sync.dma_start(out=x_sb[:, :, 0:512], in_=x_v[0][:, :, 0:512])
+        nc.sync.dma_start(out=x_sb[:, :, 512:HW], in_=x_v[0][:, :, 512:HW])
+        rb_b = vec_load(nc.scalar, rsign_bias, "rb_b")
+        gam_b = vec_load(nc.scalar, bn_gamma, "gam_b")
+        mean_b = vec_load(nc.scalar, bn_mean, "mean_b")
+        beta_b = vec_load(nc.scalar, bn_beta, "beta_b")
         for b in range(1, B):
-            nc.sync.dma_start(out=x_t[b][:], in_=x_v[b])
+            nc.sync.dma_start(out=x_sb[:, :, b * HW : (b + 1) * HW], in_=x_v[b])
 
-        grp = []
-        for g in range(2):
-            gt = consts.tile([P, PADW, J], BF16, name="grp%d" % g, align_bytes=64)
-            nc.vector.memset(gt[:, HW:PADW, :], 0.0)
-            grp.append(gt)
+        def small(name):
+            return consts.tile([P, J], F32, name=name)
 
-        ve = consts.tile([P, J], F32, name="ve")
+        ve = small("ve")
         nc.vector.tensor_scalar(out=ve[:], in0=var_b[:], scalar1=BN_EPS, scalar2=None, op0=ALU.add)
-        sq = consts.tile([P, J], F32, name="sq")
+        sq = small("sq")
         nc.scalar.activation(out=sq[:], in_=ve[:], func=ACT.Sqrt)
-        rstd = consts.tile([P, J], F32, name="rstd")
-        nc.vector.reciprocal(out=rstd[:], in_=sq[:])
-        a_c = consts.tile([P, J], F32, name="a_c")
-        nc.vector.tensor_tensor(out=a_c[:], in0=gam_b[:], in1=rstd[:], op=ALU.mult)
-        am = consts.tile([P, J], F32, name="am")
-        nc.vector.tensor_tensor(out=am[:], in0=a_c[:], in1=mean_b[:], op=ALU.mult)
-        k1 = consts.tile([P, J], F32, name="k1")
-        nc.vector.tensor_tensor(out=k1[:], in0=beta_b[:], in1=am[:], op=ALU.subtract)
-        k2 = consts.tile([P, J], F32, name="k2")
-        nc.vector.tensor_tensor(out=k2[:], in0=k1[:], in1=shift_b[:], op=ALU.subtract)
-        k_c = consts.tile([P, J], F32, name="k_c")
-        nc.vector.tensor_tensor(out=k_c[:], in0=k2[:], in1=pb_b[:], op=ALU.add)
-        pb_c = consts.tile([P, J], F32, name="pb_c")
-        nc.vector.tensor_copy(out=pb_c[:], in_=pb_b[:])
-        c_c = consts.tile([P, J], F32, name="c_c")
-        nc.vector.tensor_scalar(
-            out=c_c[:], in0=slope_b[:], scalar1=-1.0, scalar2=1.0, op0=ALU.mult, op1=ALU.add
-        )
+        codes = consts.tile([P, N], U32, name="codes", align_bytes=64)
+        scl = consts.tile([P, N], U8, name="scl", align_bytes=64)
+        d_t = {}
+        g_t = {}
+        z_t = {}
+        q_t = {}
 
-        wmean = consts.tile([P, J], F32, name="wmean")
+        def shift_x(k):
+            n0, width = starts[k], CHUNKS[k]
+            d_t[k] = dpool.tile([P, J, 1024], BF16, name="dt_")
+            for j in range(J):
+                nc.vector.tensor_scalar(
+                    out=d_t[k][:, j, 0:width], in0=x_sb[:, j, n0 : n0 + width],
+                    scalar1=rb_b[:, j : j + 1], scalar2=None, op0=ALU.add,
+                )
+
+        def sign_group(k):
+            g_t[k] = gpool.tile([P, 1024, J], BF16, name="gt", align_bytes=64)
+            for c0, c1 in pieces(CHUNKS[k]):
+                nc.scalar.activation(
+                    out=g_t[k][:, c0:c1, :].rearrange("p (c i) t -> p c t i", i=4),
+                    in_=d_t[k][:, :, c0:c1].rearrange("p t (c i) -> p c t i", i=4),
+                    func=ACT.Sign,
+                )
+
+        def quantise(k):
+            n0 = starts[k]
+            flat = g_t[k][:].rearrange("p w t -> p (w t)")
+            for c0, c1 in pieces(CHUNKS[k]):
+                nc.vector.quantize_mx(
+                    out=codes[:, n0 + c0 : n0 + c1].bitcast(FP8X4),
+                    scales=scl[:, n0 + c0 : n0 + c1],
+                    in_=flat[:, 4 * c0 : 4 * c1],
+                )
+
+        def residual_g(k):
+            n0, width = starts[k], CHUNKS[k]
+            z_t[k] = zpool.tile([P, J, 1024], F32, name="zt")
+            for j in range(G_UNITS):
+                nc.gpsimd.tensor_scalar(
+                    out=z_t[k][:, j, 0:width], in0=x_sb[:, j, n0 : n0 + width], scalar1=1.0,
+                    scalar2=k_c[:, j : j + 1], op0=ALU.mult, op1=ALU.add,
+                )
+
+        def residual_s(k):
+            n0, width = starts[k], CHUNKS[k]
+            for j in range(G_UNITS, J):
+                nc.scalar.activation(
+                    out=z_t[k][:, j, 0:width], in_=x_sb[:, j, n0 : n0 + width], func=ACT.Identity,
+                    bias=k_c[:, j : j + 1], scale=1.0,
+                )
+
+        def multiply(k):
+            n0 = starts[k]
+            zt = z_t[k]
+            for c0, c1 in pieces(CHUNKS[k]):
+                for j in range(J):
+                    wcols = slice(j * P, (j + 1) * P)
+                    acc = psum.tile([P, 512], F32, name="acc", tag="acc")
+                    nc.tensor.matmul_mx(
+                        out=acc[:, 0 : c1 - c0],
+                        lhsT=w_codes[:, wcols].bitcast(FP8X4),
+                        lhsT_scale=w_scl[:, wcols],
+                        rhs=codes[:, n0 + c0 : n0 + c1].bitcast(FP8X4),
+                        rhs_scale=scl[:, n0 + c0 : n0 + c1],
+                        start=True,
+                        stop=True,
+                    )
+                    nc.vector.scalar_tensor_tensor(
+                        out=zt[:, j, c0:c1], in0=acc[:, 0 : c1 - c0], scalar=a_c[:, j : j + 1],
+                        in1=zt[:, j, c0:c1], op0=ALU.mult, op1=ALU.add,
+                    )
+
+        def negative_part(k):
+            width = CHUNKS[k]
+            for j in range(J):
+                q_t[(k, j)] = qpool.tile([P, 1024], F32, name="qt", tag="qt")
+                nc.scalar.activation(
+                    out=q_t[(k, j)][:, 0:width], in_=z_t[k][:, j, 0:width], func=ACT.Relu,
+                    bias=pb_c[:, j : j + 1], scale=-1.0,
+                )
+
+        def finish(k):
+            n0, width = starts[k], CHUNKS[k]
+            zt = z_t[k]
+            for j in range(J):
+                nc.vector.scalar_tensor_tensor(
+                    out=zt[:, j, 0:width], in0=q_t[(k, j)][:, 0:width], scalar=c_c[:, j : j + 1],
+                    in1=zt[:, j, 0:width], op0=ALU.mult, op1=ALU.add,
+                )
+                for b in range(B):
+                    lo = max(n0, b * HW)
+                    hi = min(n0 + width, (b + 1) * HW)
+                    if lo < hi:
+                        nc.sync.dma_start(
+                            out=out_v[b][:, j, lo - b * HW : hi - b * HW],
+                            in_=zt[:, j, lo - n0 : hi - n0],
+                        )
+
+        wmean = small("wmean")
         wabs = consts.tile([P, C], BF16, name="wabs")
-        sgn = consts.tile([P, J, C], BF16, name="sgn")
-        wb = consts.tile([P, J, J, P], BF16, name="wb")
         g_w = consts.tile([P, J, P, J], BF16, name="g_w", align_bytes=64)
         w_codes = consts.tile([P, C], U32, name="w_codes", align_bytes=64)
         w_scl = consts.tile([P, C], U8, name="w_scl", align_bytes=64)
-        w_flat = w_sb[:].rearrange("p j i -> p (j i)")
-        w_gt = consts.tile([P, J * C], BF16, name="w_gt")
-        w_lt = consts.tile([P, J * C], BF16, name="w_lt")
-        nc.vector.tensor_scalar(out=w_gt[:], in0=w_flat, scalar1=0.0, scalar2=None, op0=ALU.is_gt)
-        nc.vector.tensor_scalar(out=w_lt[:], in0=w_flat, scalar1=0.0, scalar2=None, op0=ALU.is_lt)
-        nc.vector.tensor_tensor(
-            out=sgn[:].rearrange("p j i -> p (j i)"), in0=w_gt[:], in1=w_lt[:], op=ALU.subtract
-        )
         for j in range(J):
             nc.scalar.activation(
                 out=wabs[:], in_=w_sb[:, j, :], func=ACT.Abs, scale=1.0 / C,
                 accum_out=wmean[:, j : j + 1],
             )
+        w_flat = w_sb[:].rearrange("p j i -> p (j i)")
+        w_gt = qpool.tile([P, J * C], BF16, name="w_gt", tag="qt")
+        w_lt = qpool.tile([P, J * C], BF16, name="w_lt", tag="qt")
+        sgn = qpool.tile([P, J, C], BF16, name="sgn", tag="qt")
+        wb = qpool.tile([P, J, J, P], BF16, name="wb", tag="qt")
+        nc.vector.tensor_scalar(out=w_gt[:], in0=w_flat, scalar1=0.0, scalar2=None, op0=ALU.is_gt)
+        nc.vector.tensor_scalar(out=w_lt[:], in0=w_flat, scalar1=0.0, scalar2=None, op0=ALU.is_lt)
+        nc.vector.tensor_tensor(
+            out=sgn[:].rearrange("p j i -> p (j i)"), in0=w_gt[:], in1=w_lt[:], op=ALU.subtract
+        )
+        shift_x(0)
+        sign_group(0)
+        rstd = small("rstd")
+        nc.vector.reciprocal(out=rstd[:], in_=sq[:])
+        a_c = small("a_c")
+        nc.vector.tensor_tensor(out=a_c[:], in0=gam_b[:], in1=rstd[:], op=ALU.mult)
+        am = small("am")
+        nc.vector.tensor_tensor(out=am[:], in0=a_c[:], in1=mean_b[:], op=ALU.mult)
+        k1 = small("k1")
+        nc.vector.tensor_tensor(out=k1[:], in0=beta_b[:], in1=am[:], op=ALU.subtract)
+        k2 = small("k2")
+        nc.vector.tensor_tensor(out=k2[:], in0=k1[:], in1=shift_b[:], op=ALU.subtract)
+        k_c = small("k_c")
+        nc.vector.tensor_tensor(out=k_c[:], in0=k2[:], in1=pb_b[:], op=ALU.add)
+        w_T = []
         for j in range(J):
             nc.vector.tensor_scalar(
                 out=wb[:, j], in0=sgn[:, j, :].rearrange("p (q t) -> p t q", t=J),
@@ -128,7 +218,14 @@ def tile_lowerblock_kernel(
             wT = psum.tile([P, J, P], BF16, name="wT", tag="acc")
             for t in range(J):
                 nc.tensor.transpose(wT[:, t, :], wb[:, j, t, :], ident[:])
-            nc.vector.tensor_copy(out=g_w[:, j], in_=wT[:].rearrange("p t r -> p r t"))
+            w_T.append(wT)
+        shift_x(1)
+        for j in range(J):
+            src = w_T[j][:].rearrange("p t r -> p r t")
+            if j < 2:
+                nc.vector.tensor_copy(out=g_w[:, j], in_=src)
+            else:
+                nc.scalar.copy(out=g_w[:, j], in_=src)
         for j in range(J):
             cols = slice(j * P, (j + 1) * P)
             nc.vector.quantize_mx(
@@ -136,93 +233,27 @@ def tile_lowerblock_kernel(
                 scales=w_scl[:, cols],
                 in_=g_w[:, j].rearrange("p r t -> p (r t)"),
             )
+        residual_g(0)
+        residual_s(0)
+        quantise(0)
+        pb_c = small("pb_c")
+        nc.vector.tensor_copy(out=pb_c[:], in_=pb_b[:])
+        c_c = small("c_c")
+        nc.vector.tensor_scalar(
+            out=c_c[:], in0=slope_b[:], scalar1=-1.0, scalar2=1.0, op0=ALU.mult, op1=ALU.add
+        )
 
-        codes = consts.tile([P, B, PADW], U32, name="codes", align_bytes=64)
-        scl = consts.tile([P, B, PADW], U8, name="scl", align_bytes=64)
-        z_t = {}
-
-        def front(b):
-            xt = x_t[b]
-            dt_ = dpool.tile([P, J, HW], BF16, name="dt_")
-            for j in range(J):
-                nc.vector.tensor_scalar(
-                    out=dt_[:, j, :], in0=xt[:, j, :], scalar1=rb_b[:, j : j + 1], scalar2=None,
-                    op0=ALU.add,
-                )
-            gt = grp[b % 2]
-            for c0, c1 in ((0, 512), (512, HW)):
-                nc.scalar.activation(
-                    out=gt[:, c0:c1, :].rearrange("p (c i) t -> p c t i", i=4),
-                    in_=dt_[:, :, c0:c1].rearrange("p t (c i) -> p c t i", i=4),
-                    func=ACT.Sign,
-                )
-            flat = gt[:].rearrange("p w t -> p (w t)")
-            for c0, c1 in ((0, 512), (512, 768), (768, 896)):
-                nc.vector.quantize_mx(
-                    out=codes[:, b, c0:c1].bitcast(FP8X4),
-                    scales=scl[:, b, c0:c1],
-                    in_=flat[:, 4 * c0 : 4 * c1],
-                )
-            zt = zpool.tile([P, J, HW], F32, name="zt")
-            for j in range(J):
-                if b < 4:
-                    nc.vector.tensor_scalar(
-                        out=zt[:, j, :], in0=xt[:, j, :], scalar1=k_c[:, j : j + 1], scalar2=None,
-                        op0=ALU.add,
-                    )
-                else:
-                    nc.scalar.activation(
-                        out=zt[:, j, :], in_=xt[:, j, :], func=ACT.Identity,
-                        bias=k_c[:, j : j + 1], scale=1.0,
-                    )
-            z_t[b] = zt
-
-        def mx(acc, j, b, c0, c1):
-            wcols = slice(j * P, (j + 1) * P)
-            nc.tensor.matmul_mx(
-                out=acc,
-                lhsT=w_codes[:, wcols].bitcast(FP8X4),
-                lhsT_scale=w_scl[:, wcols],
-                rhs=codes[:, b, c0:c1].bitcast(FP8X4),
-                rhs_scale=scl[:, b, c0:c1],
-                start=True,
-                stop=True,
-            )
-
-        def back(b):
-            zt = z_t[b]
-            qt = qpool.tile([P, J, HW], F32, name="qt")
-            for j in range(J):
-                acc_a = psum.tile([P, 512], F32, name="acc_a", tag="acc")
-                acc_b = psum.tile([P, 512], F32, name="acc_b", tag="acc")
-                mx(acc_a[:], j, b, 0, 512)
-                mx(acc_b[:, 0:256], j, b, 512, 768)
-                mx(acc_b[:, 256:384], j, b, 768, 896)
-                nc.vector.scalar_tensor_tensor(
-                    out=zt[:, j, 0:512], in0=acc_a[:], scalar=a_c[:, j : j + 1],
-                    in1=zt[:, j, 0:512], op0=ALU.mult, op1=ALU.add,
-                )
-                nc.vector.scalar_tensor_tensor(
-                    out=zt[:, j, 512:HW], in0=acc_b[:, 0 : HW - 512], scalar=a_c[:, j : j + 1],
-                    in1=zt[:, j, 512:HW], op0=ALU.mult, op1=ALU.add,
-                )
-                nc.scalar.activation(
-                    out=qt[:, j, :], in_=zt[:, j, :], func=ACT.Relu, bias=pb_c[:, j : j + 1],
-                    scale=-1.0,
-                )
-            for j in range(J):
-                nc.vector.scalar_tensor_tensor(
-                    out=zt[:, j, :], in0=qt[:, j, :], scalar=c_c[:, j : j + 1],
-                    in1=zt[:, j, :], op0=ALU.mult, op1=ALU.add,
-                )
-                if b == B - 1:
-                    nc.sync.dma_start(out=out_v[b][:, j, :], in_=zt[:, j, :])
-            if b < B - 1:
-                nc.sync.dma_start(out=out_v[b], in_=zt[:])
-
-        front(0)
-        front(1)
-        for b in range(B):
-            if b + 2 < B:
-                front(b + 2)
-            back(b)
+        for k in range(n_chunks):
+            if k + 1 < n_chunks:
+                residual_g(k + 1)
+                sign_group(k + 1)
+                residual_s(k + 1)
+            multiply(k)
+            if k + 2 < n_chunks:
+                shift_x(k + 2)
+            if k + 1 < n_chunks:
+                quantise(k + 1)
+            if k >= 1:
+                finish(k - 1)
+            negative_part(k)
+        finish(n_chunks - 1)

@@ -18,8 +18,10 @@ C = 512
 HW = 784
 N = B * HW
 CHUNKS = (512, 1024, 1024, 1024, 1024, 1024, 640)
-G_UNITS = 3
+G_UNITS = (4, 4, 3, 3, 3, 3, 3)
 BN_EPS = 1e-5
+GAIN_A = 73786976294838206464.0
+GAIN_B = 147573952589676412928.0
 FLOPS = 2 * C * C * B * HW
 
 
@@ -40,7 +42,7 @@ def tile_lowerblock_kernel(
         consts = ctx.enter_context(tc.tile_pool(name="consts", bufs=1))
         dpool = ctx.enter_context(tc.tile_pool(name="dpool", bufs=2))
         gpool = ctx.enter_context(tc.tile_pool(name="gpool", bufs=2))
-        zpool = ctx.enter_context(tc.tile_pool(name="zpool", bufs=4))
+        zpool = ctx.enter_context(tc.tile_pool(name="zpool", bufs=16))
         qpool = ctx.enter_context(tc.tile_pool(name="qpool", bufs=6))
         psum = ctx.enter_context(tc.psum_pool(name="psum", bufs=8))
         ctx.enter_context(tc.manual_schedule())
@@ -113,26 +115,27 @@ def tile_lowerblock_kernel(
 
         def residual_g(k):
             n0, width = starts[k], CHUNKS[k]
-            z_t[k] = zpool.tile([P, J, 1024], F32, name="zt")
-            for j in range(G_UNITS):
+            for j in range(G_UNITS[k]):
+                z_t[(k, j)] = zpool.tile([P, 1024], F32, name="zt", tag="zt")
                 nc.gpsimd.tensor_scalar(
-                    out=z_t[k][:, j, 0:width], in0=x_sb[:, j, n0 : n0 + width], scalar1=1.0,
+                    out=z_t[(k, j)][:, 0:width], in0=x_sb[:, j, n0 : n0 + width], scalar1=1.0,
                     scalar2=k_c[:, j : j + 1], op0=ALU.mult, op1=ALU.add,
                 )
 
         def residual_s(k):
             n0, width = starts[k], CHUNKS[k]
-            for j in range(G_UNITS, J):
+            for j in range(G_UNITS[k], J):
+                z_t[(k, j)] = zpool.tile([P, 1024], F32, name="zt", tag="zt")
                 nc.scalar.activation(
-                    out=z_t[k][:, j, 0:width], in_=x_sb[:, j, n0 : n0 + width], func=ACT.Identity,
-                    bias=k_c[:, j : j + 1], scale=1.0,
+                    out=z_t[(k, j)][:, 0:width], in_=x_sb[:, j, n0 : n0 + width],
+                    func=ACT.Identity, bias=k_c[:, j : j + 1], scale=1.0,
                 )
 
         def multiply(k):
             n0 = starts[k]
-            zt = z_t[k]
             for c0, c1 in pieces(CHUNKS[k]):
                 for j in range(J):
+                    zt = z_t[(k, j)]
                     wcols = slice(j * P, (j + 1) * P)
                     acc = psum.tile([P, 512], F32, name="acc", tag="acc")
                     nc.tensor.matmul_mx(
@@ -145,8 +148,8 @@ def tile_lowerblock_kernel(
                         stop=True,
                     )
                     nc.vector.scalar_tensor_tensor(
-                        out=zt[:, j, c0:c1], in0=acc[:, 0 : c1 - c0], scalar=a_c[:, j : j + 1],
-                        in1=zt[:, j, c0:c1], op0=ALU.mult, op1=ALU.add,
+                        out=zt[:, c0:c1], in0=acc[:, 0 : c1 - c0], scalar=a_c[:, j : j + 1],
+                        in1=zt[:, c0:c1], op0=ALU.mult, op1=ALU.add,
                     )
 
         def negative_part(k):
@@ -154,17 +157,17 @@ def tile_lowerblock_kernel(
             for j in range(J):
                 q_t[(k, j)] = qpool.tile([P, 1024], F32, name="qt", tag="qt")
                 nc.scalar.activation(
-                    out=q_t[(k, j)][:, 0:width], in_=z_t[k][:, j, 0:width], func=ACT.Relu,
+                    out=q_t[(k, j)][:, 0:width], in_=z_t[(k, j)][:, 0:width], func=ACT.Relu,
                     bias=pb_c[:, j : j + 1], scale=-1.0,
                 )
 
         def finish(k):
             n0, width = starts[k], CHUNKS[k]
-            zt = z_t[k]
             for j in range(J):
+                zt = z_t[(k, j)]
                 nc.vector.scalar_tensor_tensor(
-                    out=zt[:, j, 0:width], in0=q_t[(k, j)][:, 0:width], scalar=c_c[:, j : j + 1],
-                    in1=zt[:, j, 0:width], op0=ALU.mult, op1=ALU.add,
+                    out=zt[:, 0:width], in0=q_t[(k, j)][:, 0:width], scalar=c_c[:, j : j + 1],
+                    in1=zt[:, 0:width], op0=ALU.mult, op1=ALU.add,
                 )
                 for b in range(B):
                     lo = max(n0, b * HW)
@@ -172,7 +175,7 @@ def tile_lowerblock_kernel(
                     if lo < hi:
                         nc.sync.dma_start(
                             out=out_v[b][:, j, lo - b * HW : hi - b * HW],
-                            in_=zt[:, j, lo - n0 : hi - n0],
+                            in_=zt[:, lo - n0 : hi - n0],
                         )
 
         wmean = small("wmean")
@@ -186,29 +189,40 @@ def tile_lowerblock_kernel(
                 accum_out=wmean[:, j : j + 1],
             )
         w_flat = w_sb[:].rearrange("p j i -> p (j i)")
-        w_gt = qpool.tile([P, J * C], BF16, name="w_gt", tag="qt")
-        w_lt = qpool.tile([P, J * C], BF16, name="w_lt", tag="qt")
+        w_big = qpool.tile([P, J * C], BF16, name="w_big", tag="qt")
+        w_big2 = qpool.tile([P, J * C], BF16, name="w_big2", tag="qt")
         sgn = qpool.tile([P, J, C], BF16, name="sgn", tag="qt")
         wb = qpool.tile([P, J, J, P], BF16, name="wb", tag="qt")
-        nc.vector.tensor_scalar(out=w_gt[:], in0=w_flat, scalar1=0.0, scalar2=None, op0=ALU.is_gt)
-        nc.vector.tensor_scalar(out=w_lt[:], in0=w_flat, scalar1=0.0, scalar2=None, op0=ALU.is_lt)
-        nc.vector.tensor_tensor(
-            out=sgn[:].rearrange("p j i -> p (j i)"), in0=w_gt[:], in1=w_lt[:], op=ALU.subtract
+        nc.vector.tensor_scalar(
+            out=w_big[:], in0=w_flat, scalar1=GAIN_A, scalar2=1.0, op0=ALU.mult, op1=ALU.min
+        )
+        nc.vector.tensor_scalar(
+            out=w_big2[:], in0=w_big[:], scalar1=-1.0, scalar2=GAIN_B, op0=ALU.max, op1=ALU.mult
+        )
+        nc.vector.tensor_scalar(
+            out=sgn[:].rearrange("p j i -> p (j i)"), in0=w_big2[:], scalar1=1.0, scalar2=-1.0,
+            op0=ALU.min, op1=ALU.max,
         )
         shift_x(0)
         sign_group(0)
         rstd = small("rstd")
         nc.vector.reciprocal(out=rstd[:], in_=sq[:])
         a_c = small("a_c")
-        nc.vector.tensor_tensor(out=a_c[:], in0=gam_b[:], in1=rstd[:], op=ALU.mult)
+        nc.gpsimd.tensor_tensor(out=a_c[:], in0=gam_b[:], in1=rstd[:], op=ALU.mult)
         am = small("am")
-        nc.vector.tensor_tensor(out=am[:], in0=a_c[:], in1=mean_b[:], op=ALU.mult)
+        nc.gpsimd.tensor_tensor(out=am[:], in0=a_c[:], in1=mean_b[:], op=ALU.mult)
         k1 = small("k1")
-        nc.vector.tensor_tensor(out=k1[:], in0=beta_b[:], in1=am[:], op=ALU.subtract)
+        nc.gpsimd.tensor_tensor(out=k1[:], in0=beta_b[:], in1=am[:], op=ALU.subtract)
         k2 = small("k2")
-        nc.vector.tensor_tensor(out=k2[:], in0=k1[:], in1=shift_b[:], op=ALU.subtract)
+        nc.gpsimd.tensor_tensor(out=k2[:], in0=k1[:], in1=shift_b[:], op=ALU.subtract)
         k_c = small("k_c")
-        nc.vector.tensor_tensor(out=k_c[:], in0=k2[:], in1=pb_b[:], op=ALU.add)
+        nc.gpsimd.tensor_tensor(out=k_c[:], in0=k2[:], in1=pb_b[:], op=ALU.add)
+        pb_c = small("pb_c")
+        nc.gpsimd.tensor_copy(out=pb_c[:], in_=pb_b[:])
+        c_c = small("c_c")
+        nc.gpsimd.tensor_scalar(
+            out=c_c[:], in0=slope_b[:], scalar1=-1.0, scalar2=1.0, op0=ALU.mult, op1=ALU.add
+        )
         w_T = []
         for j in range(J):
             nc.vector.tensor_scalar(
@@ -236,12 +250,6 @@ def tile_lowerblock_kernel(
         residual_g(0)
         residual_s(0)
         quantise(0)
-        pb_c = small("pb_c")
-        nc.vector.tensor_copy(out=pb_c[:], in_=pb_b[:])
-        c_c = small("c_c")
-        nc.vector.tensor_scalar(
-            out=c_c[:], in0=slope_b[:], scalar1=-1.0, scalar2=1.0, op0=ALU.mult, op1=ALU.add
-        )
 
         for k in range(n_chunks):
             if k + 1 < n_chunks:

@@ -18,7 +18,7 @@ C = 512
 HW = 784
 N = B * HW
 CHUNKS = (512, 1024, 1024, 1024, 1024, 1024, 640)
-G_UNITS = (4, 4, 3, 3, 3, 3, 3)
+G_UNITS = 3
 BN_EPS = 1e-5
 GAIN_A = 73786976294838206464.0
 GAIN_B = 147573952589676412928.0
@@ -42,7 +42,7 @@ def tile_lowerblock_kernel(
         consts = ctx.enter_context(tc.tile_pool(name="consts", bufs=1))
         dpool = ctx.enter_context(tc.tile_pool(name="dpool", bufs=2))
         gpool = ctx.enter_context(tc.tile_pool(name="gpool", bufs=2))
-        zpool = ctx.enter_context(tc.tile_pool(name="zpool", bufs=16))
+        zpool = ctx.enter_context(tc.tile_pool(name="zpool", bufs=4))
         qpool = ctx.enter_context(tc.tile_pool(name="qpool", bufs=6))
         psum = ctx.enter_context(tc.psum_pool(name="psum", bufs=8))
         ctx.enter_context(tc.manual_schedule())
@@ -52,22 +52,22 @@ def tile_lowerblock_kernel(
             queue.dma_start(out=t[:], in_=v.rearrange("(p j) -> p j", j=J))
             return t
 
-        shift_b = vec_load(nc.gpsimd, pr_shift, "shift_b")
-        pb_b = vec_load(nc.gpsimd, pr_bias, "pb_b")
+        rb_b = vec_load(nc.gpsimd, rsign_bias, "rb_b")
         slope_b = vec_load(nc.gpsimd, pr_slope, "slope_b")
         ident = consts.tile([P, P], BF16, name="ident")
         make_identity(nc, ident[:])
 
         var_b = vec_load(nc.scalar, bn_var, "var_b")
+        gam_b = vec_load(nc.scalar, bn_gamma, "gam_b")
+        mean_b = vec_load(nc.scalar, bn_mean, "mean_b")
+        beta_b = vec_load(nc.scalar, bn_beta, "beta_b")
+        shift_b = vec_load(nc.scalar, pr_shift, "shift_b")
+        pb_b = vec_load(nc.scalar, pr_bias, "pb_b")
         w_sb = consts.tile([P, J, C], BF16, name="w_sb")
         x_sb = consts.tile([P, J, N], BF16, name="x_sb")
         nc.sync.dma_start(out=w_sb[:], in_=W.rearrange("(p j) i -> p j i", j=J))
         nc.sync.dma_start(out=x_sb[:, :, 0:512], in_=x_v[0][:, :, 0:512])
         nc.sync.dma_start(out=x_sb[:, :, 512:HW], in_=x_v[0][:, :, 512:HW])
-        rb_b = vec_load(nc.scalar, rsign_bias, "rb_b")
-        gam_b = vec_load(nc.scalar, bn_gamma, "gam_b")
-        mean_b = vec_load(nc.scalar, bn_mean, "mean_b")
-        beta_b = vec_load(nc.scalar, bn_beta, "beta_b")
         for b in range(1, B):
             nc.sync.dma_start(out=x_sb[:, :, b * HW : (b + 1) * HW], in_=x_v[b])
 
@@ -78,6 +78,23 @@ def tile_lowerblock_kernel(
         nc.vector.tensor_scalar(out=ve[:], in0=var_b[:], scalar1=BN_EPS, scalar2=None, op0=ALU.add)
         sq = small("sq")
         nc.scalar.activation(out=sq[:], in_=ve[:], func=ACT.Sqrt)
+        rstd = small("rstd")
+        nc.vector.reciprocal(out=rstd[:], in_=sq[:])
+        a_c = small("a_c")
+        nc.vector.tensor_tensor(out=a_c[:], in0=gam_b[:], in1=rstd[:], op=ALU.mult)
+        am = small("am")
+        nc.vector.tensor_tensor(out=am[:], in0=a_c[:], in1=mean_b[:], op=ALU.mult)
+        k1 = small("k1")
+        nc.vector.tensor_tensor(out=k1[:], in0=beta_b[:], in1=am[:], op=ALU.subtract)
+        k2 = small("k2")
+        nc.vector.tensor_tensor(out=k2[:], in0=k1[:], in1=shift_b[:], op=ALU.subtract)
+        k_c = small("k_c")
+        nc.vector.tensor_tensor(out=k_c[:], in0=k2[:], in1=pb_b[:], op=ALU.add)
+        pb_c = small("pb_c")
+        nc.vector.tensor_copy(out=pb_c[:], in_=pb_b[:])
+        nbc = small("nbc")
+        nc.vector.tensor_scalar(out=nbc[:], in0=k2[:], scalar1=-1.0, scalar2=None, op0=ALU.mult)
+        tok = consts.tile([P, 8], F32, name="tok")
         codes = consts.tile([P, N], U32, name="codes", align_bytes=64)
         scl = consts.tile([P, N], U8, name="scl", align_bytes=64)
         d_t = {}
@@ -115,27 +132,28 @@ def tile_lowerblock_kernel(
 
         def residual_g(k):
             n0, width = starts[k], CHUNKS[k]
-            for j in range(G_UNITS[k]):
-                z_t[(k, j)] = zpool.tile([P, 1024], F32, name="zt", tag="zt")
+            z_t[k] = zpool.tile([P, J, 1024], F32, name="zt")
+            for j in range(G_UNITS):
                 nc.gpsimd.tensor_scalar(
-                    out=z_t[(k, j)][:, 0:width], in0=x_sb[:, j, n0 : n0 + width], scalar1=1.0,
-                    scalar2=k_c[:, j : j + 1], op0=ALU.mult, op1=ALU.add,
+                    out=z_t[k][:, j, 0:width], in0=x_sb[:, j, n0 : n0 + width],
+                    scalar1=tok[:, k - 1 : k], scalar2=k_c[:, j : j + 1], op0=ALU.mult, op1=ALU.add,
                 )
 
         def residual_s(k):
             n0, width = starts[k], CHUNKS[k]
-            for j in range(G_UNITS[k], J):
-                z_t[(k, j)] = zpool.tile([P, 1024], F32, name="zt", tag="zt")
+            for j in range(G_UNITS, J):
                 nc.scalar.activation(
-                    out=z_t[(k, j)][:, 0:width], in_=x_sb[:, j, n0 : n0 + width],
-                    func=ACT.Identity, bias=k_c[:, j : j + 1], scale=1.0,
+                    out=z_t[k][:, j, 0:width], in_=x_sb[:, j, n0 : n0 + width], func=ACT.Identity,
+                    bias=k_c[:, j : j + 1], scale=1.0,
                 )
 
         def multiply(k):
             n0 = starts[k]
+            if k == 0:
+                z_t[k] = zpool.tile([P, J, 1024], F32, name="zt")
+            zt = z_t[k]
             for c0, c1 in pieces(CHUNKS[k]):
                 for j in range(J):
-                    zt = z_t[(k, j)]
                     wcols = slice(j * P, (j + 1) * P)
                     acc = psum.tile([P, 512], F32, name="acc", tag="acc")
                     nc.tensor.matmul_mx(
@@ -147,35 +165,49 @@ def tile_lowerblock_kernel(
                         start=True,
                         stop=True,
                     )
+                    res = x_sb[:, j, n0 + c0 : n0 + c1] if k == 0 else zt[:, j, c0:c1]
                     nc.vector.scalar_tensor_tensor(
-                        out=zt[:, c0:c1], in0=acc[:, 0 : c1 - c0], scalar=a_c[:, j : j + 1],
-                        in1=zt[:, c0:c1], op0=ALU.mult, op1=ALU.add,
+                        out=zt[:, j, c0:c1], in0=acc[:, 0 : c1 - c0], scalar=a_c[:, j : j + 1],
+                        in1=res, op0=ALU.mult, op1=ALU.add,
                     )
 
         def negative_part(k):
             width = CHUNKS[k]
             for j in range(J):
                 q_t[(k, j)] = qpool.tile([P, 1024], F32, name="qt", tag="qt")
-                nc.scalar.activation(
-                    out=q_t[(k, j)][:, 0:width], in_=z_t[(k, j)][:, 0:width], func=ACT.Relu,
-                    bias=pb_c[:, j : j + 1], scale=-1.0,
-                )
+                if k == 0:
+                    nc.vector.tensor_scalar(
+                        out=q_t[(k, j)][:, 0:width], in0=z_t[k][:, j, 0:width],
+                        scalar1=nbc[:, j : j + 1], scalar2=negc[:, j : j + 1],
+                        op0=ALU.min, op1=ALU.mult,
+                    )
+                else:
+                    nc.scalar.activation(
+                        out=q_t[(k, j)][:, 0:width], in_=z_t[k][:, j, 0:width], func=ACT.Relu,
+                        bias=pb_c[:, j : j + 1], scale=-1.0,
+                    )
 
         def finish(k):
             n0, width = starts[k], CHUNKS[k]
+            zt = z_t[k]
             for j in range(J):
-                zt = z_t[(k, j)]
-                nc.vector.scalar_tensor_tensor(
-                    out=zt[:, 0:width], in0=q_t[(k, j)][:, 0:width], scalar=c_c[:, j : j + 1],
-                    in1=zt[:, 0:width], op0=ALU.mult, op1=ALU.add,
-                )
+                if k == 0:
+                    nc.vector.scalar_tensor_tensor(
+                        out=zt[:, j, 0:width], in0=zt[:, j, 0:width], scalar=kap[:, j : j + 1],
+                        in1=q_t[(k, j)][:, 0:width], op0=ALU.add, op1=ALU.add,
+                    )
+                else:
+                    nc.vector.scalar_tensor_tensor(
+                        out=zt[:, j, 0:width], in0=q_t[(k, j)][:, 0:width],
+                        scalar=c_c[:, j : j + 1], in1=zt[:, j, 0:width], op0=ALU.mult, op1=ALU.add,
+                    )
                 for b in range(B):
                     lo = max(n0, b * HW)
                     hi = min(n0 + width, (b + 1) * HW)
                     if lo < hi:
                         nc.sync.dma_start(
                             out=out_v[b][:, j, lo - b * HW : hi - b * HW],
-                            in_=zt[:, lo - n0 : hi - n0],
+                            in_=zt[:, j, lo - n0 : hi - n0],
                         )
 
         wmean = small("wmean")
@@ -205,24 +237,6 @@ def tile_lowerblock_kernel(
         )
         shift_x(0)
         sign_group(0)
-        rstd = small("rstd")
-        nc.vector.reciprocal(out=rstd[:], in_=sq[:])
-        a_c = small("a_c")
-        nc.gpsimd.tensor_tensor(out=a_c[:], in0=gam_b[:], in1=rstd[:], op=ALU.mult)
-        am = small("am")
-        nc.gpsimd.tensor_tensor(out=am[:], in0=a_c[:], in1=mean_b[:], op=ALU.mult)
-        k1 = small("k1")
-        nc.gpsimd.tensor_tensor(out=k1[:], in0=beta_b[:], in1=am[:], op=ALU.subtract)
-        k2 = small("k2")
-        nc.gpsimd.tensor_tensor(out=k2[:], in0=k1[:], in1=shift_b[:], op=ALU.subtract)
-        k_c = small("k_c")
-        nc.gpsimd.tensor_tensor(out=k_c[:], in0=k2[:], in1=pb_b[:], op=ALU.add)
-        pb_c = small("pb_c")
-        nc.gpsimd.tensor_copy(out=pb_c[:], in_=pb_b[:])
-        c_c = small("c_c")
-        nc.gpsimd.tensor_scalar(
-            out=c_c[:], in0=slope_b[:], scalar1=-1.0, scalar2=1.0, op0=ALU.mult, op1=ALU.add
-        )
         w_T = []
         for j in range(J):
             nc.vector.tensor_scalar(
@@ -247,12 +261,21 @@ def tile_lowerblock_kernel(
                 scales=w_scl[:, cols],
                 in_=g_w[:, j].rearrange("p r t -> p (r t)"),
             )
-        residual_g(0)
-        residual_s(0)
         quantise(0)
+        c_c = small("c_c")
+        nc.vector.tensor_scalar(
+            out=c_c[:], in0=slope_b[:], scalar1=-1.0, scalar2=1.0, op0=ALU.mult, op1=ALU.add
+        )
+        negc = small("negc")
+        nc.vector.tensor_scalar(out=negc[:], in0=slope_b[:], scalar1=-1.0, scalar2=None, op0=ALU.add)
+        ck = small("ck")
+        nc.vector.tensor_tensor(out=ck[:], in0=negc[:], in1=k2[:], op=ALU.mult)
+        kap = small("kap")
+        nc.vector.tensor_tensor(out=kap[:], in0=k_c[:], in1=ck[:], op=ALU.add)
 
         for k in range(n_chunks):
             if k + 1 < n_chunks:
+                nc.vector.memset(tok[:, k : k + 1], 1.0)
                 residual_g(k + 1)
                 sign_group(k + 1)
                 residual_s(k + 1)
@@ -261,7 +284,9 @@ def tile_lowerblock_kernel(
                 shift_x(k + 2)
             if k + 1 < n_chunks:
                 quantise(k + 1)
-            if k >= 1:
+            if k >= 2:
                 finish(k - 1)
             negative_part(k)
+            if k == 0:
+                finish(0)
         finish(n_chunks - 1)

@@ -52,22 +52,22 @@ def tile_lowerblock_kernel(
             queue.dma_start(out=t[:], in_=v.rearrange("(p j) -> p j", j=J))
             return t
 
-        rb_b = vec_load(nc.gpsimd, rsign_bias, "rb_b")
+        shift_b = vec_load(nc.gpsimd, pr_shift, "shift_b")
+        pb_b = vec_load(nc.gpsimd, pr_bias, "pb_b")
         slope_b = vec_load(nc.gpsimd, pr_slope, "slope_b")
         ident = consts.tile([P, P], BF16, name="ident")
         make_identity(nc, ident[:])
 
         var_b = vec_load(nc.scalar, bn_var, "var_b")
-        gam_b = vec_load(nc.scalar, bn_gamma, "gam_b")
-        mean_b = vec_load(nc.scalar, bn_mean, "mean_b")
-        beta_b = vec_load(nc.scalar, bn_beta, "beta_b")
-        shift_b = vec_load(nc.scalar, pr_shift, "shift_b")
-        pb_b = vec_load(nc.scalar, pr_bias, "pb_b")
         w_sb = consts.tile([P, J, C], BF16, name="w_sb")
         x_sb = consts.tile([P, J, N], BF16, name="x_sb")
         nc.sync.dma_start(out=w_sb[:], in_=W.rearrange("(p j) i -> p j i", j=J))
         nc.sync.dma_start(out=x_sb[:, :, 0:512], in_=x_v[0][:, :, 0:512])
         nc.sync.dma_start(out=x_sb[:, :, 512:HW], in_=x_v[0][:, :, 512:HW])
+        rb_b = vec_load(nc.scalar, rsign_bias, "rb_b")
+        gam_b = vec_load(nc.scalar, bn_gamma, "gam_b")
+        mean_b = vec_load(nc.scalar, bn_mean, "mean_b")
+        beta_b = vec_load(nc.scalar, bn_beta, "beta_b")
         for b in range(1, B):
             nc.sync.dma_start(out=x_sb[:, :, b * HW : (b + 1) * HW], in_=x_v[b])
 
@@ -78,22 +78,6 @@ def tile_lowerblock_kernel(
         nc.vector.tensor_scalar(out=ve[:], in0=var_b[:], scalar1=BN_EPS, scalar2=None, op0=ALU.add)
         sq = small("sq")
         nc.scalar.activation(out=sq[:], in_=ve[:], func=ACT.Sqrt)
-        rstd = small("rstd")
-        nc.vector.reciprocal(out=rstd[:], in_=sq[:])
-        a_c = small("a_c")
-        nc.vector.tensor_tensor(out=a_c[:], in0=gam_b[:], in1=rstd[:], op=ALU.mult)
-        am = small("am")
-        nc.vector.tensor_tensor(out=am[:], in0=a_c[:], in1=mean_b[:], op=ALU.mult)
-        k1 = small("k1")
-        nc.vector.tensor_tensor(out=k1[:], in0=beta_b[:], in1=am[:], op=ALU.subtract)
-        k2 = small("k2")
-        nc.vector.tensor_tensor(out=k2[:], in0=k1[:], in1=shift_b[:], op=ALU.subtract)
-        k_c = small("k_c")
-        nc.vector.tensor_tensor(out=k_c[:], in0=k2[:], in1=pb_b[:], op=ALU.add)
-        pb_c = small("pb_c")
-        nc.vector.tensor_copy(out=pb_c[:], in_=pb_b[:])
-        nbc = small("nbc")
-        nc.vector.tensor_scalar(out=nbc[:], in0=k2[:], scalar1=-1.0, scalar2=None, op0=ALU.mult)
         tok = consts.tile([P, 8], F32, name="tok")
         codes = consts.tile([P, N], U32, name="codes", align_bytes=64)
         scl = consts.tile([P, N], U8, name="scl", align_bytes=64)
@@ -237,6 +221,22 @@ def tile_lowerblock_kernel(
         )
         shift_x(0)
         sign_group(0)
+        rstd = small("rstd")
+        nc.vector.reciprocal(out=rstd[:], in_=sq[:])
+        a_c = small("a_c")
+        nc.vector.tensor_tensor(out=a_c[:], in0=gam_b[:], in1=rstd[:], op=ALU.mult)
+        am = small("am")
+        nc.vector.tensor_tensor(out=am[:], in0=a_c[:], in1=mean_b[:], op=ALU.mult)
+        k1 = small("k1")
+        nc.vector.tensor_tensor(out=k1[:], in0=beta_b[:], in1=am[:], op=ALU.subtract)
+        k2 = small("k2")
+        nc.vector.tensor_tensor(out=k2[:], in0=k1[:], in1=shift_b[:], op=ALU.subtract)
+        k_c = small("k_c")
+        nc.vector.tensor_tensor(out=k_c[:], in0=k2[:], in1=pb_b[:], op=ALU.add)
+        pb_c = small("pb_c")
+        nc.vector.tensor_copy(out=pb_c[:], in_=pb_b[:])
+        nbc = small("nbc")
+        nc.vector.tensor_scalar(out=nbc[:], in0=k2[:], scalar1=-1.0, scalar2=None, op0=ALU.mult)
         w_T = []
         for j in range(J):
             nc.vector.tensor_scalar(

@@ -208,7 +208,7 @@ def tile_lowerblock_kernel(
         w_big = qpool.tile([P, J * C], BF16, name="w_big", tag="qt")
         w_big2 = qpool.tile([P, J * C], BF16, name="w_big2", tag="qt")
         sgn = qpool.tile([P, J, C], BF16, name="sgn", tag="qt")
-        wb = qpool.tile([P, J, J, P], BF16, name="wb", tag="qt")
+        diag = qpool.tile([P, J, P], BF16, name="diag", tag="qt")
         nc.vector.tensor_scalar(
             out=w_big[:], in0=w_flat, scalar1=GAIN_A, scalar2=1.0, op0=ALU.mult, op1=ALU.min
         )
@@ -224,28 +224,42 @@ def tile_lowerblock_kernel(
         rstd = small("rstd")
         nc.vector.reciprocal(out=rstd[:], in_=sq[:])
         a_c = small("a_c")
-        nc.vector.tensor_tensor(out=a_c[:], in0=gam_b[:], in1=rstd[:], op=ALU.mult)
+        nc.gpsimd.tensor_tensor(out=a_c[:], in0=gam_b[:], in1=rstd[:], op=ALU.mult)
         am = small("am")
-        nc.vector.tensor_tensor(out=am[:], in0=a_c[:], in1=mean_b[:], op=ALU.mult)
+        nc.gpsimd.tensor_tensor(out=am[:], in0=a_c[:], in1=mean_b[:], op=ALU.mult)
         k1 = small("k1")
-        nc.vector.tensor_tensor(out=k1[:], in0=beta_b[:], in1=am[:], op=ALU.subtract)
+        nc.gpsimd.tensor_tensor(out=k1[:], in0=beta_b[:], in1=am[:], op=ALU.subtract)
         k2 = small("k2")
-        nc.vector.tensor_tensor(out=k2[:], in0=k1[:], in1=shift_b[:], op=ALU.subtract)
+        nc.gpsimd.tensor_tensor(out=k2[:], in0=k1[:], in1=shift_b[:], op=ALU.subtract)
         k_c = small("k_c")
-        nc.vector.tensor_tensor(out=k_c[:], in0=k2[:], in1=pb_b[:], op=ALU.add)
+        nc.gpsimd.tensor_tensor(out=k_c[:], in0=k2[:], in1=pb_b[:], op=ALU.add)
         pb_c = small("pb_c")
-        nc.vector.tensor_copy(out=pb_c[:], in_=pb_b[:])
+        nc.gpsimd.tensor_copy(out=pb_c[:], in_=pb_b[:])
         nbc = small("nbc")
-        nc.vector.tensor_scalar(out=nbc[:], in0=k2[:], scalar1=-1.0, scalar2=None, op0=ALU.mult)
+        nc.gpsimd.tensor_scalar(out=nbc[:], in0=k2[:], scalar1=-1.0, scalar2=0.0, op0=ALU.mult, op1=ALU.add)
+        c_c = small("c_c")
+        nc.gpsimd.tensor_scalar(
+            out=c_c[:], in0=slope_b[:], scalar1=-1.0, scalar2=1.0, op0=ALU.mult, op1=ALU.add
+        )
+        negc = small("negc")
+        nc.gpsimd.tensor_scalar(
+            out=negc[:], in0=slope_b[:], scalar1=1.0, scalar2=-1.0, op0=ALU.mult, op1=ALU.add
+        )
+        ck = small("ck")
+        nc.gpsimd.tensor_tensor(out=ck[:], in0=negc[:], in1=k2[:], op=ALU.mult)
+        kap = small("kap")
+        nc.gpsimd.tensor_tensor(out=kap[:], in0=k_c[:], in1=ck[:], op=ALU.add)
         w_T = []
         for j in range(J):
             nc.vector.tensor_scalar(
-                out=wb[:, j], in0=sgn[:, j, :].rearrange("p (q t) -> p t q", t=J),
-                scalar1=wmean[:, j : j + 1], scalar2=None, op0=ALU.mult,
+                out=diag[:, j, :], in0=ident[:], scalar1=wmean[:, j : j + 1], scalar2=None, op0=ALU.mult,
             )
             wT = psum.tile([P, J, P], BF16, name="wT", tag="acc")
+            sgn_t = sgn[:, j, :].rearrange("p (q t) -> p t q", t=J)
             for t in range(J):
-                nc.tensor.transpose(wT[:, t, :], wb[:, j, t, :], ident[:])
+                nc.tensor.matmul(
+                    out=wT[:, t, :], lhsT=sgn_t[:, t, :], rhs=diag[:, j, :], start=True, stop=True
+                )
             w_T.append(wT)
         shift_x(1)
         for j in range(J):
@@ -262,16 +276,6 @@ def tile_lowerblock_kernel(
                 in_=g_w[:, j].rearrange("p r t -> p (r t)"),
             )
         quantise(0)
-        c_c = small("c_c")
-        nc.vector.tensor_scalar(
-            out=c_c[:], in0=slope_b[:], scalar1=-1.0, scalar2=1.0, op0=ALU.mult, op1=ALU.add
-        )
-        negc = small("negc")
-        nc.vector.tensor_scalar(out=negc[:], in0=slope_b[:], scalar1=-1.0, scalar2=None, op0=ALU.add)
-        ck = small("ck")
-        nc.vector.tensor_tensor(out=ck[:], in0=negc[:], in1=k2[:], op=ALU.mult)
-        kap = small("kap")
-        nc.vector.tensor_tensor(out=kap[:], in0=k_c[:], in1=ck[:], op=ALU.add)
 
         for k in range(n_chunks):
             if k + 1 < n_chunks:

@@ -118,17 +118,19 @@ def tile_lowerblock_kernel(
             n0, width = starts[k], CHUNKS[k]
             z_t[k] = zpool.tile([P, J, 1024], F32, name="zt")
             for j in range(G_UNITS):
+                g_end = width if j < G_UNITS - 1 else width // 2
                 nc.gpsimd.tensor_scalar(
-                    out=z_t[k][:, j, 0:width], in0=x_sb[:, j, n0 : n0 + width],
+                    out=z_t[k][:, j, 0:g_end], in0=x_sb[:, j, n0 : n0 + g_end],
                     scalar1=tok[:, k - 1 : k], scalar2=k_c[:, j : j + 1], op0=ALU.mult, op1=ALU.add,
                 )
 
         def residual_s(k):
             n0, width = starts[k], CHUNKS[k]
-            for j in range(G_UNITS, J):
+            for j in range(G_UNITS - 1, J):
+                s_from = 0 if j >= G_UNITS else width // 2
                 nc.scalar.activation(
-                    out=z_t[k][:, j, 0:width], in_=x_sb[:, j, n0 : n0 + width], func=ACT.Identity,
-                    bias=k_c[:, j : j + 1], scale=1.0,
+                    out=z_t[k][:, j, s_from:width], in_=x_sb[:, j, n0 + s_from : n0 + width],
+                    func=ACT.Identity, bias=k_c[:, j : j + 1], scale=1.0,
                 )
 
         def multiply(k):

@@ -278,16 +278,17 @@ def tile_lowerblock_kernel(
                 in_=g_w[:, j].rearrange("p r t -> p (r t)"),
             )
         quantise(0)
+        sign_group(1)
 
         for k in range(n_chunks):
             if k + 1 < n_chunks:
                 nc.vector.memset(tok[:, k : k + 1], 1.0)
                 residual_g(k + 1)
-                sign_group(k + 1)
                 residual_s(k + 1)
             multiply(k)
             if k + 2 < n_chunks:
                 shift_x(k + 2)
+                sign_group(k + 2)
             if k + 1 < n_chunks:
                 quantise(k + 1)
             if k >= 2:

@@ -279,14 +279,17 @@ def tile_lowerblock_kernel(
             )
         quantise(0)
         sign_group(1)
+        shift_x(2)
 
         for k in range(n_chunks):
             if k + 1 < n_chunks:
                 nc.vector.memset(tok[:, k : k + 1], 1.0)
                 residual_g(k + 1)
                 residual_s(k + 1)
+            if k == 0:
+                sign_group(2)
             multiply(k)
-            if k + 2 < n_chunks:
+            if 0 < k and k + 2 < n_chunks:
                 shift_x(k + 2)
                 sign_group(k + 2)
             if k + 1 < n_chunks:

@@ -282,16 +282,15 @@ def tile_lowerblock_kernel(
         shift_x(2)
 
         for k in range(n_chunks):
+            if 0 < k and k + 2 < n_chunks:
+                shift_x(k + 2)
             if k + 1 < n_chunks:
                 nc.vector.memset(tok[:, k : k + 1], 1.0)
                 residual_g(k + 1)
                 residual_s(k + 1)
-            if k == 0:
-                sign_group(2)
-            multiply(k)
-            if 0 < k and k + 2 < n_chunks:
-                shift_x(k + 2)
+            if k + 2 < n_chunks:
                 sign_group(k + 2)
+            multiply(k)
             if k + 1 < n_chunks:
                 quantise(k + 1)
             if k >= 2:

@@ -43,7 +43,7 @@ def tile_lowerblock_kernel(
         dpool = ctx.enter_context(tc.tile_pool(name="dpool", bufs=2))
         gpool = ctx.enter_context(tc.tile_pool(name="gpool", bufs=2))
         zpool = ctx.enter_context(tc.tile_pool(name="zpool", bufs=4))
-        qpool = ctx.enter_context(tc.tile_pool(name="qpool", bufs=6))
+        qpool = ctx.enter_context(tc.tile_pool(name="qpool", bufs=8))
         psum = ctx.enter_context(tc.psum_pool(name="psum", bufs=8))
         ctx.enter_context(tc.manual_schedule())
 
@@ -107,7 +107,7 @@ def tile_lowerblock_kernel(
         def quantise(k):
             n0 = starts[k]
             flat = g_t[k][:].rearrange("p w t -> p (w t)")
-            for c0, c1 in pieces(CHUNKS[k]):
+            for c0, c1 in ([(0, 1024)] if (CHUNKS[k] == 1024 and k >= 2) else pieces(CHUNKS[k])):
                 nc.vector.quantize_mx(
                     out=codes[:, n0 + c0 : n0 + c1].bitcast(FP8X4),
                     scales=scl[:, n0 + c0 : n0 + c1],

from contextlib import ExitStack

import concourse.mybir as mybir
from concourse.masks import make_identity

F32 = mybir.dt.float32
BF16 = mybir.dt.bfloat16
U32 = mybir.dt.uint32
U8 = mybir.dt.uint8
FP8X4 = mybir.dt.float8_e4m3fn_x4
ACT = mybir.ActivationFunctionType
ALU = mybir.AluOpType

P = 128
J = 4
B = 8
C = 512
HW = 784
N = B * HW
CHUNKS = (512, 1024, 1024, 1024, 1024, 1024, 640)
G_UNITS = 3
BN_EPS = 1e-5
GAIN_A = 73786976294838206464.0
GAIN_B = 147573952589676412928.0
FLOPS = 2 * C * C * B * HW


def tile_lowerblock_kernel(
    tc, x, rsign_bias, W, bn_gamma, bn_beta, bn_mean, bn_var, pr_slope, pr_shift, pr_bias, out
):
    nc = tc.nc
    x_v = x.rearrange("b (p j) h w -> b p j (h w)", j=J)
    out_v = out.rearrange("b (p j) h w -> b p j (h w)", j=J)
    n_chunks = len(CHUNKS)
    starts = [sum(CHUNKS[:k]) for k in range(n_chunks)]

    def pieces(width):
        cuts = list(range(0, width, 512)) + [width]
        return list(zip(cuts[:-1], cuts[1:]))

    with ExitStack() as ctx:
        consts = ctx.enter_context(tc.tile_pool(name="consts", bufs=1))
        dpool = ctx.enter_context(tc.tile_pool(name="dpool", bufs=2))
        gpool = ctx.enter_context(tc.tile_pool(name="gpool", bufs=2))
        zpool = ctx.enter_context(tc.tile_pool(name="zpool", bufs=4))
        qpool = ctx.enter_context(tc.tile_pool(name="qpool", bufs=8))
        psum = ctx.enter_context(tc.psum_pool(name="psum", bufs=8))
        ctx.enter_context(tc.manual_schedule())

        def vec_load(queue, v, name):
            t = consts.tile([P, J], BF16, name=name)
            queue.dma_start(out=t[:], in_=v.rearrange("(p j) -> p j", j=J))
            return t

        shift_b = vec_load(nc.gpsimd, pr_shift, "shift_b")
        pb_b = vec_load(nc.gpsimd, pr_bias, "pb_b")
        slope_b = vec_load(nc.gpsimd, pr_slope, "slope_b")
        ident = consts.tile([P, P], BF16, name="ident")
        make_identity(nc, ident[:])

        var_b = vec_load(nc.scalar, bn_var, "var_b")
        w_sb = consts.tile([P, J, C], BF16, name="w_sb")
        x_sb = consts.tile([P, J, N], BF16, name="x_sb")
        nc.sync.dma_start(out=w_sb[:], in_=W.rearrange("(p j) i -> p j i", j=J))
        nc.sync.dma_start(out=x_sb[:, :, 0:512], in_=x_v[0][:, :, 0:512])
        nc.sync.dma_start(out=x_sb[:, :, 512:HW], in_=x_v[0][:, :, 512:HW])
        rb_b = vec_load(nc.scalar, rsign_bias, "rb_b")
        gam_b = vec_load(nc.scalar, bn_gamma, "gam_b")
        mean_b = vec_load(nc.scalar, bn_mean, "mean_b")
        beta_b = vec_load(nc.scalar, bn_beta, "beta_b")
        for b in range(1, B):
            nc.sync.dma_start(out=x_sb[:, :, b * HW : (b + 1) * HW], in_=x_v[b])

        def small(name):
            return consts.tile([P, J], F32, name=name)

        ve = small("ve")
        nc.vector.tensor_scalar(out=ve[:], in0=var_b[:], scalar1=BN_EPS, scalar2=None, op0=ALU.add)
        sq = small("sq")
        nc.scalar.activation(out=sq[:], in_=ve[:], func=ACT.Sqrt)
        tok = consts.tile([P, 8], F32, name="tok")
        codes = consts.tile([P, N], U32, name="codes", align_bytes=64)
        scl = consts.tile([P, N], U8, name="scl", align_bytes=64)
        d_t = {}
        g_t = {}
        z_t = {}
        q_t = {}

        def shift_x(k):
            n0, width = starts[k], CHUNKS[k]
            d_t[k] = dpool.tile([P, J, 1024], BF16, name="dt_")
            for j in range(J):
                nc.vector.tensor_scalar(
                    out=d_t[k][:, j, 0:width], in0=x_sb[:, j, n0 : n0 + width],
                    scalar1=rb_b[:, j : j + 1], scalar2=None, op0=ALU.add,
                )

        def sign_group(k):
            g_t[k] = gpool.tile([P, 1024, J], BF16, name="gt", align_bytes=64)
            for c0, c1 in pieces(CHUNKS[k]):
                nc.scalar.activation(
                    out=g_t[k][:, c0:c1, :].rearrange("p (c i) t -> p c t i", i=4),
                    in_=d_t[k][:, :, c0:c1].rearrange("p t (c i) -> p c t i", i=4),
                    func=ACT.Sign,
                )

        def quantise(k):
            n0 = starts[k]
            flat = g_t[k][:].rearrange("p w t -> p (w t)")
            for c0, c1 in ([(0, 1024)] if (CHUNKS[k] == 1024 and k >= 2) else pieces(CHUNKS[k])):
                nc.vector.quantize_mx(
                    out=codes[:, n0 + c0 : n0 + c1].bitcast(FP8X4),
                    scales=scl[:, n0 + c0 : n0 + c1],
                    in_=flat[:, 4 * c0 : 4 * c1],
                )

        def residual_g(k):
            n0, width = starts[k], CHUNKS[k]
            z_t[k] = zpool.tile([P, J, 1024], F32, name="zt")
            for j in range(G_UNITS):
                g_end = width if j < G_UNITS - 1 else width // 2
                nc.gpsimd.tensor_scalar(
                    out=z_t[k][:, j, 0:g_end], in0=x_sb[:, j, n0 : n0 + g_end],
                    scalar1=tok[:, k - 1 : k], scalar2=k_c[:, j : j + 1], op0=ALU.mult, op1=ALU.add,
                )

        def residual_s(k):
            n0, width = starts[k], CHUNKS[k]
            for j in range(G_UNITS - 1, J):
                s_from = 0 if j >= G_UNITS else width // 2
                nc.scalar.activation(
                    out=z_t[k][:, j, s_from:width], in_=x_sb[:, j, n0 + s_from : n0 + width],
                    func=ACT.Identity, bias=k_c[:, j : j + 1], scale=1.0,
                )

        def multiply(k):
            n0 = starts[k]
            if k == 0:
                z_t[k] = zpool.tile([P, J, 1024], F32, name="zt")
            zt = z_t[k]
            for c0, c1 in pieces(CHUNKS[k]):
                for j in range(J):
                    wcols = slice(j * P, (j + 1) * P)
                    acc = psum.tile([P, 512], F32, name="acc", tag="acc")
                    nc.tensor.matmul_mx(
                        out=acc[:, 0 : c1 - c0],
                        lhsT=w_codes[:, wcols].bitcast(FP8X4),
                        lhsT_scale=w_scl[:, wcols],
                        rhs=codes[:, n0 + c0 : n0 + c1].bitcast(FP8X4),
                        rhs_scale=scl[:, n0 + c0 : n0 + c1],
                        start=True,
                        stop=True,
                    )
                    res = x_sb[:, j, n0 + c0 : n0 + c1] if k == 0 else zt[:, j, c0:c1]
                    nc.vector.scalar_tensor_tensor(
                        out=zt[:, j, c0:c1], in0=acc[:, 0 : c1 - c0], scalar=a_c[:, j : j + 1],
                        in1=res, op0=ALU.mult, op1=ALU.add,
                    )

        def negative_part(k):
            width = CHUNKS[k]
            for j in range(J):
                q_t[(k, j)] = qpool.tile([P, 1024], F32, name="qt", tag="qt")
                if k == 0:
                    nc.vector.tensor_scalar(
                        out=q_t[(k, j)][:, 0:width], in0=z_t[k][:, j, 0:width],
                        scalar1=nbc[:, j : j + 1], scalar2=negc[:, j : j + 1],
                        op0=ALU.min, op1=ALU.mult,
                    )
                else:
                    nc.scalar.activation(
                        out=q_t[(k, j)][:, 0:width], in_=z_t[k][:, j, 0:width], func=ACT.Relu,
                        bias=pb_c[:, j : j + 1], scale=-1.0,
                    )

        def finish(k):
            n0, width = starts[k], CHUNKS[k]
            zt = z_t[k]
            for j in range(J):
                if k == 0:
                    nc.vector.scalar_tensor_tensor(
                        out=zt[:, j, 0:width], in0=zt[:, j, 0:width], scalar=kap[:, j : j + 1],
                        in1=q_t[(k, j)][:, 0:width], op0=ALU.add, op1=ALU.add,
                    )
                else:
                    nc.vector.scalar_tensor_tensor(
                        out=zt[:, j, 0:width], in0=q_t[(k, j)][:, 0:width],
                        scalar=c_c[:, j : j + 1], in1=zt[:, j, 0:width], op0=ALU.mult, op1=ALU.add,
                    )
                for b in range(B):
                    lo = max(n0, b * HW)
                    hi = min(n0 + width, (b + 1) * HW)
                    if lo < hi:
                        nc.sync.dma_start(
                            out=out_v[b][:, j, lo - b * HW : hi - b * HW],
                            in_=zt[:, j, lo - n0 : hi - n0],
                        )

        wmean = small("wmean")
        wabs = consts.tile([P, C], BF16, name="wabs")
        g_w = consts.tile([P, J, P, J], BF16, name="g_w", align_bytes=64)
        w_codes = consts.tile([P, C], U32, name="w_codes", align_bytes=64)
        w_scl = consts.tile([P, C], U8, name="w_scl", align_bytes=64)
        for j in range(J):
            nc.scalar.activation(
                out=wabs[:], in_=w_sb[:, j, :], func=ACT.Abs, scale=1.0 / C,
                accum_out=wmean[:, j : j + 1],
            )
        w_flat = w_sb[:].rearrange("p j i -> p (j i)")
        w_big = qpool.tile([P, J * C], BF16, name="w_big", tag="qt")
        w_big2 = qpool.tile([P, J * C], BF16, name="w_big2", tag="qt")
        sgn = qpool.tile([P, J, C], BF16, name="sgn", tag="qt")
        diag = qpool.tile([P, J, P], BF16, name="diag", tag="qt")
        nc.vector.tensor_scalar(
            out=w_big[:], in0=w_flat, scalar1=GAIN_A, scalar2=1.0, op0=ALU.mult, op1=ALU.min
        )
        nc.vector.tensor_scalar(
            out=w_big2[:], in0=w_big[:], scalar1=-1.0, scalar2=GAIN_B, op0=ALU.max, op1=ALU.mult
        )
        nc.vector.tensor_scalar(
            out=sgn[:].rearrange("p j i -> p (j i)"), in0=w_big2[:], scalar1=1.0, scalar2=-1.0,
            op0=ALU.min, op1=ALU.max,
        )
        shift_x(0)
        sign_group(0)
        rstd = small("rstd")
        nc.vector.reciprocal(out=rstd[:], in_=sq[:])
        a_c = small("a_c")
        nc.gpsimd.tensor_tensor(out=a_c[:], in0=gam_b[:], in1=rstd[:], op=ALU.mult)
        am = small("am")
        nc.gpsimd.tensor_tensor(out=am[:], in0=a_c[:], in1=mean_b[:], op=ALU.mult)
        k1 = small("k1")
        nc.gpsimd.tensor_tensor(out=k1[:], in0=beta_b[:], in1=am[:], op=ALU.subtract)
        k2 = small("k2")
        nc.gpsimd.tensor_tensor(out=k2[:], in0=k1[:], in1=shift_b[:], op=ALU.subtract)
        k_c = small("k_c")
        nc.gpsimd.tensor_tensor(out=k_c[:], in0=k2[:], in1=pb_b[:], op=ALU.add)
        pb_c = small("pb_c")
        nc.gpsimd.tensor_copy(out=pb_c[:], in_=pb_b[:])
        nbc = small("nbc")
        nc.gpsimd.tensor_scalar(out=nbc[:], in0=k2[:], scalar1=-1.0, scalar2=0.0, op0=ALU.mult, op1=ALU.add)
        c_c = small("c_c")
        nc.gpsimd.tensor_scalar(
            out=c_c[:], in0=slope_b[:], scalar1=-1.0, scalar2=1.0, op0=ALU.mult, op1=ALU.add
        )
        negc = small("negc")
        nc.gpsimd.tensor_scalar(
            out=negc[:], in0=slope_b[:], scalar1=1.0, scalar2=-1.0, op0=ALU.mult, op1=ALU.add
        )
        ck = small("ck")
        nc.gpsimd.tensor_tensor(out=ck[:], in0=negc[:], in1=k2[:], op=ALU.mult)
        kap = small("kap")
        nc.gpsimd.tensor_tensor(out=kap[:], in0=k_c[:], in1=ck[:], op=ALU.add)
        w_T = []
        for j in range(J):
            nc.vector.tensor_scalar(
                out=diag[:, j, :], in0=ident[:], scalar1=wmean[:, j : j + 1], scalar2=None, op0=ALU.mult,
            )
            wT = psum.tile([P, J, P], BF16, name="wT", tag="acc")
            sgn_t = sgn[:, j, :].rearrange("p (q t) -> p t q", t=J)
            for t in range(J):
                nc.tensor.matmul(
                    out=wT[:, t, :], lhsT=sgn_t[:, t, :], rhs=diag[:, j, :], start=True, stop=True
                )
            w_T.append(wT)
        shift_x(1)
        for j in range(J):
            src = w_T[j][:].rearrange("p t r -> p r t")
            if j < 2:
                nc.vector.tensor_copy(out=g_w[:, j], in_=src)
            else:
                nc.scalar.copy(out=g_w[:, j], in_=src)
        for j in range(J):
            cols = slice(j * P, (j + 1) * P)
            nc.vector.quantize_mx(
                out=w_codes[:, cols].bitcast(FP8X4),
                scales=w_scl[:, cols],
                in_=g_w[:, j].rearrange("p r t -> p (r t)"),
            )
        quantise(0)
        sign_group(1)
        shift_x(2)

        for k in range(n_chunks):
            if 0 < k and k + 2 < n_chunks:
                shift_x(k + 2)
            if k + 1 < n_chunks:
                nc.vector.memset(tok[:, k : k + 1], 1.0)
                residual_g(k + 1)
                residual_s(k + 1)
            if k + 2 < n_chunks:
                sign_group(k + 2)
            multiply(k)
            if k + 1 < n_chunks:
                quantise(k + 1)
            if k >= 2:
                finish(k - 1)
            negative_part(k)
            if k == 0:
                finish(0)
        finish(n_chunks - 1)
